import numpy as np
import ml_dtypes


def mxq(x, axis, fmt="e4m3"):
    dtype, down = {"e4m3": (ml_dtypes.float8_e4m3fn, 7), "e5m2": (ml_dtypes.float8_e5m2, 14)}[fmt]
    v = np.moveaxis(np.asarray(x, np.float32).astype(ml_dtypes.bfloat16).astype(np.float64), axis, -1)
    blocks = v.reshape(v.shape[:-1] + (-1, 32))
    amax = np.abs(blocks).max(-1, keepdims=True)
    byte = np.maximum(np.where(amax > 0, np.frexp(amax)[1] - 1 + 127, 0) - down, 1)
    scale = np.exp2(byte - 127.0)
    codes = (blocks / scale).astype(np.float32).astype(dtype).astype(np.float64)
    return np.moveaxis((codes * scale).reshape(v.shape), -1, axis)


WIDE = False


def mx_kscale(k):
    if not WIDE:
        return np.ones(k)
    levels = np.array([10, -10, 5, -5, 0])
    a = np.random.permutation(np.resize(levels, k // 512 * 4)).reshape(k // 512, 4)
    idx = np.arange(k)
    return np.exp2(a[idx // 512, idx % 128 // 32])


BF16 = ml_dtypes.bfloat16


def bf(x):
    return np.asarray(x, np.float32).astype(BF16)


def f64(x):
    return np.asarray(x).astype(np.float64)


B, T, D, H, DH, R, F = 1, 512, 1024, 4, 256, 64, 4096
EPS = 1e-5
E = H * DH


def rope(u, c, s):
    ur, up = u[..., :R], u[..., R:]
    c = c[None, :, None, :]
    s = s[None, :, None, :]
    ue, uo = ur[..., ::2], ur[..., 1::2]
    ur2 = np.stack([ue * c - uo * s, uo * c + ue * s], axis=-1).reshape(ur.shape)
    return np.concatenate([ur2, up], axis=-1)


def setup_inputs():
    rn = np.random.standard_normal
    s = mx_kscale(D)
    ang = np.random.uniform(0.0, 2.0 * np.pi, (T, R // 2))
    return {
        "x": bf(3.0 * np.sqrt(EPS) * (rn((B, T, D)) + 0.5 * rn((B, T, 1)))),
        "ln_scale": bf((1.0 + 0.1 * rn(D)) * s),
        "ln_offset": bf(0.1 * rn(D) * s),
        "wq": bf(rn((D, E)) / np.sqrt(D) / s[:, None]),
        "wk": bf(rn((D, E)) / np.sqrt(D) / s[:, None]),
        "wv": bf(rn((D, E)) / np.sqrt(D) / s[:, None]),
        "rope_cos": bf(np.cos(ang)),
        "rope_sin": bf(np.sin(ang)),
    }


def reference(x, ln_scale, ln_offset, wq, wk, wv, rope_cos, rope_sin):
    x = f64(x)
    mean = x.mean(-1, keepdims=True)
    var = ((x - mean) ** 2).mean(-1, keepdims=True)
    xn = (x - mean) * (1.0 / np.sqrt(var + EPS))
    xn = xn * f64(ln_scale) + f64(ln_offset)
    xq = mxq(xn, 2, "e4m3")
    q = (xq @ mxq(f64(wq), 0, "e4m3")).reshape(B, T, H, DH)
    k = (xq @ mxq(f64(wk), 0, "e4m3")).reshape(B, T, H, DH)
    v = (xq @ mxq(f64(wv), 0, "e4m3")).reshape(B, T, H, DH)
    c, s = f64(rope_cos), f64(rope_sin)
    return rope(q, c, s), rope(k, c, s), v

@@ -1,0 +1,265 @@
+from contextlib import ExitStack
+
+import concourse.mybir as mybir
+from concourse.masks import make_identity
+
+F32 = mybir.dt.float32
+BF16 = mybir.dt.bfloat16
+I32 = mybir.dt.int32
+U32 = mybir.dt.uint32
+U8 = mybir.dt.uint8
+FP8X4 = mybir.dt.float8_e4m3fn_x4
+ALU = mybir.AluOpType
+
+P = 128
+TOKENS = 512
+D_MODEL = 1024
+HEADS = 4
+HEAD_DIM = 256
+ROTATED = 64
+PAIRS = ROTATED // 2
+WIDTH = HEADS * HEAD_DIM
+EPS = 1e-5
+
+TOKEN_TILES = TOKENS // P
+PACK = 4
+K_PASS = P * PACK
+PASSES = D_MODEL // K_PASS
+BANK = 512
+HALF_HEAD = HEAD_DIM // 2
+STATS_WIDTH = 512
+STATS_DIM = 6
+QUARTER = WIDTH // 4
+EARLY_CHUNKS = 4
+
+FLOPS = 2 * TOKENS * D_MODEL * 3 * WIDTH
+
+
+def tile_transformerlayershard_pa_kernel(
+    tc, x, ln_scale, ln_offset, wq, wk, wv, rope_cos, rope_sin, out_0, out_1, out_2
+):
+    nc = tc.nc
+    projections = [(wq, out_0, True), (wv, out_2, False), (wk, out_1, True)]
+    chunks = len(projections) * PASSES
+
+    with ExitStack() as stack:
+        keep = stack.enter_context(tc.tile_pool(name="keep", bufs=1))
+        per_tile = stack.enter_context(tc.tile_pool(name="per_tile", bufs=TOKEN_TILES))
+        banks = stack.enter_context(tc.psum_pool(name="banks", bufs=8))
+        stack.enter_context(tc.manual_schedule())
+
+        cos_bf = keep.tile([P, TOKEN_TILES, PAIRS], BF16)
+        sin_bf = keep.tile([P, TOKEN_TILES, PAIRS], BF16)
+        nc.scalar.dma_start(out=cos_bf[:], in_=rope_cos.rearrange("(p a) i -> p a i", a=TOKEN_TILES))
+        nc.scalar.dma_start(out=sin_bf[:], in_=rope_sin.rearrange("(p a) i -> p a i", a=TOKEN_TILES))
+
+        x_rows = x.flatten_outer_dims().rearrange("(p a) d -> p a d", a=TOKEN_TILES)
+        x_sb = keep.tile([P, TOKEN_TILES, D_MODEL], BF16)
+        for first in range(0, TOKEN_TILES, 2):
+            nc.sync.dma_start(out=x_sb[:, first : first + 2, :], in_=x_rows[:, first : first + 2, :])
+
+        affine_rows = keep.tile([P, 2 * D_MODEL], BF16)
+        nc.vector.memset(affine_rows[:].bitcast(I32), 0)
+        nc.sync.dma_start(out=affine_rows[0:1, 0:D_MODEL], in_=ln_scale.rearrange("(o d) -> o d", o=1))
+        nc.sync.dma_start(out=affine_rows[0:1, D_MODEL : 2 * D_MODEL], in_=ln_offset.rearrange("(o d) -> o d", o=1))
+
+        w_raw = []
+        for m, (w, out, rotate) in enumerate(projections):
+            for g in range(PASSES):
+                raw = keep.tile([P, PACK, WIDTH], BF16, name="w_raw_%d_%d" % (m, g))
+                nc.sync.dma_start(
+                    out=raw[:].rearrange("q (u e) n -> q u (e n)", e=2),
+                    in_=w[g * K_PASS : (g + 1) * K_PASS, :].rearrange("(u q e) n -> q u (e n)", u=2, e=2),
+                )
+                w_raw.append(raw)
+
+        ones = keep.tile([P, P], BF16)
+        nc.vector.memset(ones[:], 1.0)
+        warm = keep.tile([P, 1], F32)
+        nc.vector.memset(warm[:], 1.0)
+        nc.scalar.sqrt(warm[:], warm[:])
+        identity = keep.tile([P, P], F32)
+        make_identity(nc, identity[:])
+
+        cos_or_one = keep.tile([P, TOKEN_TILES, HALF_HEAD], F32)
+        nc.gpsimd.memset(cos_or_one[:], 1.0)
+        nc.gpsimd.tensor_copy(
+            out=cos_or_one[:, :, 0:ROTATED].rearrange("p a (i e) -> p a i e", e=2),
+            in_=cos_bf[:].unsqueeze(3).to_broadcast([P, TOKEN_TILES, PAIRS, 2]),
+        )
+        signed_sin = keep.tile([P, TOKEN_TILES, 2, PAIRS], F32)
+        nc.gpsimd.tensor_scalar(
+            out=signed_sin[:, :, 0, :], in0=sin_bf[:], scalar1=-1.0, scalar2=0.0, op0=ALU.mult, op1=ALU.add
+        )
+        nc.gpsimd.tensor_copy(out=signed_sin[:, :, 1, :], in_=sin_bf[:])
+
+        affine_banks = []
+        for first in range(0, 2 * D_MODEL, BANK):
+            bank = banks.tile([P, BANK], F32, name="affine_%d" % first, tag="bank")
+            nc.tensor.matmul(out=bank[:], lhsT=ones[:], rhs=affine_rows[:, first : first + BANK], start=True, stop=True)
+            affine_banks.append(bank)
+        gain_banks = affine_banks[0 : D_MODEL // BANK]
+        offset_banks = affine_banks[D_MODEL // BANK :]
+
+        w_codes = keep.tile([P, chunks, WIDTH], U32, align_bytes=64)
+        w_scales = keep.tile([P, chunks, WIDTH], U8, align_bytes=64)
+        grouped = []
+        for c in range(chunks):
+            grouped.append(keep.tile([P, WIDTH, PACK], BF16, name="grouped_%d" % c, align_bytes=64))
+
+        def regroup_views(c, quarter, run):
+            cols = slice(quarter * QUARTER, (quarter + 1) * QUARTER)
+            dst = grouped[c][:, cols, :].rearrange("q (n i) t -> q n t i", i=run)
+            src = w_raw[c][:, :, cols].rearrange("q t (n i) -> q n t i", i=run)
+            return dst, src
+
+        def regroup_on_scalar(c, quarter):
+            dst, src = regroup_views(c, quarter, 4)
+            nc.scalar.copy(out=dst, in_=src)
+
+        def regroup_on_vector(c, quarter):
+            dst, src = regroup_views(c, quarter, 4)
+            nc.vector.tensor_copy(out=dst, in_=src)
+
+        def regroup_on_gpsimd(c, quarter):
+            dst, src = regroup_views(c, quarter, 1)
+            nc.gpsimd.tensor_scalar(out=dst, in0=src, scalar1=1.0, scalar2=0.0, op0=ALU.mult, op1=ALU.add)
+
+        def regroup_early(c):
+            for quarter in (0, 1):
+                regroup_on_scalar(c, quarter)
+            for quarter in (2, 3):
+                regroup_on_gpsimd(c, quarter)
+
+        def regroup_late(c):
+            for quarter in (0, 1, 2):
+                regroup_on_scalar(c, quarter)
+            regroup_on_vector(c, 3)
+
+        def quantise_weights(c):
+            nc.vector.quantize_mx(
+                out=w_codes[:, c, :].bitcast(FP8X4), scales=w_scales[:, c, :],
+                in_=grouped[c][:].rearrange("q n t -> q (n t)"),
+            )
+
+        regroup_early(0)
+
+        stats = keep.tile([P, TOKEN_TILES, D_MODEL // STATS_WIDTH, STATS_DIM], F32)
+        mean_var = keep.tile([P, TOKEN_TILES, 2], F32)
+        for a in range(TOKEN_TILES):
+            for s in range(D_MODEL // STATS_WIDTH):
+                nc.vector.bn_stats(out=stats[:, a, s, :], in_=x_sb[:, a, s * STATS_WIDTH : (s + 1) * STATS_WIDTH])
+        for a in range(TOKEN_TILES):
+            nc.vector.bn_aggr(out=mean_var[:, a, :], in_=stats[:, a, :, :].rearrange("p s v -> p (s v)"))
+        rstd = keep.tile([P, TOKEN_TILES], F32)
+        nc.vector.tensor_scalar(out=rstd[:], in0=mean_var[:, :, 1], scalar1=EPS, scalar2=None, op0=ALU.add)
+        nc.scalar.sqrt(rstd[:], rstd[:])
+
+        centred = []
+        for a in range(TOKEN_TILES):
+            centred.append(per_tile.tile([P, D_MODEL], F32, name="centred"))
+            for h, first in enumerate(range(0, D_MODEL, BANK)):
+                cols = slice(first, first + BANK)
+                nc.vector.scalar_tensor_tensor(
+                    out=centred[a][:, cols], in0=x_sb[:, a, cols], scalar=mean_var[:, a, 0:1],
+                    in1=gain_banks[h][:], op0=ALU.subtract, op1=ALU.mult,
+                )
+        nc.vector.reciprocal(rstd[:], rstd[:])
+
+        for c in range(1, EARLY_CHUNKS):
+            regroup_early(c)
+
+        x_grouped = []
+        for a in range(TOKEN_TILES):
+            xn = per_tile.tile([P, D_MODEL], BF16)
+            for h, first in enumerate(range(0, D_MODEL, BANK)):
+                cols = slice(first, first + BANK)
+                nc.vector.scalar_tensor_tensor(
+                    out=xn[:, cols], in0=centred[a][:, cols], scalar=rstd[:, a : a + 1],
+                    in1=offset_banks[h][:], op0=ALU.mult, op1=ALU.add,
+                )
+            xn_words = xn[:].bitcast(F32)
+            xt = banks.tile([P, PASSES * 2, P], F32, tag="bank")
+            for b in range(PASSES * 2):
+                nc.tensor.transpose(out=xt[:, b, :], in_=xn_words[:, b * P : (b + 1) * P], identity=identity[:])
+            x_grouped.append(per_tile.tile([P, PASSES * P * PACK], BF16, name="x_grouped", align_bytes=64))
+            nc.scalar.copy(
+                out=x_grouped[a][:].bitcast(F32).rearrange("q (g r u) -> q g r u", g=PASSES, u=2),
+                in_=xt[:].rearrange("q (g u) r -> q g r u", u=2),
+            )
+
+        x_codes = keep.tile([P, TOKEN_TILES, PASSES * P], U32, align_bytes=64)
+        x_scales = keep.tile([P, TOKEN_TILES, PASSES * P], U8, align_bytes=64)
+
+        def multiply(bank_cols, m, a, first, width):
+            for g in range(PASSES):
+                nc.tensor.matmul_mx(
+                    out=bank_cols,
+                    lhsT=x_codes[:, a, g * P : (g + 1) * P].bitcast(FP8X4),
+                    lhsT_scale=x_scales[:, a, g * P : (g + 1) * P],
+                    rhs=w_codes[:, m * PASSES + g, first : first + width].bitcast(FP8X4),
+                    rhs_scale=w_scales[:, m * PASSES + g, first : first + width],
+                    start=(g == 0),
+                    stop=(g == PASSES - 1),
+                )
+
+        def store(m, a, result):
+            out_rows = projections[m][1].flatten_outer_dims().rearrange(
+                "(p a h) d -> p a (h d)", a=TOKEN_TILES, h=HEADS
+            )
+            nc.sync.dma_start(out=out_rows[:, a, :], in_=result[:].rearrange("p h d -> p (h d)"))
+
+        def project_plain(m):
+            for a in range(TOKEN_TILES):
+                result = per_tile.tile([P, HEADS, HEAD_DIM], F32, name="result")
+                flat = result[:].rearrange("p h d -> p (h d)")
+                for first in range(0, WIDTH, BANK):
+                    bank = banks.tile([P, BANK], F32, tag="bank")
+                    multiply(bank[:], m, a, first, BANK)
+                    nc.scalar.copy(out=flat[:, first : first + BANK], in_=bank[:])
+                store(m, a, result)
+
+        def project_rotated(m):
+            products = []
+            for a in range(TOKEN_TILES + 1):
+                if a < TOKEN_TILES:
+                    leading = banks.tile([P, HEADS, HALF_HEAD], F32, tag="bank")
+                    trailing = banks.tile([P, HEADS, HALF_HEAD], F32, tag="bank")
+                    for h in range(HEADS):
+                        multiply(leading[:, h, :], m, a, h * HEAD_DIM, HALF_HEAD)
+                        multiply(trailing[:, h, :], m, a, h * HEAD_DIM + HALF_HEAD, HALF_HEAD)
+                    result = per_tile.tile([P, HEADS, HEAD_DIM], F32, name="result")
+                    cross = per_tile.tile([P, 2, HEADS, PAIRS], F32, name="cross")
+                    nc.scalar.copy(out=result[:, :, HALF_HEAD:HEAD_DIM], in_=trailing[:])
+                    nc.vector.tensor_tensor(
+                        out=result[:, :, 0:HALF_HEAD], in0=leading[:],
+                        in1=cos_or_one[:, a, :].unsqueeze(1).to_broadcast([P, HEADS, HALF_HEAD]), op=ALU.mult,
+                    )
+                    u_pairs = leading[:, :, 0:ROTATED].rearrange("p h (i e) -> p h i e", e=2)
+                    for e in range(2):
+                        nc.vector.tensor_tensor(
+                            out=cross[:, e, :, :], in0=u_pairs[:, :, :, 1 - e],
+                            in1=signed_sin[:, a, e, :].unsqueeze(1).to_broadcast([P, HEADS, PAIRS]), op=ALU.mult,
+                        )
+                    products.append((result, cross))
+                if a > 0:
+                    result, cross = products[a - 1]
+                    rotated = result[:, :, 0:ROTATED].rearrange("p h (i e) -> p h i e", e=2)
+                    nc.vector.tensor_tensor(
+                        out=rotated, in0=rotated, in1=cross[:].rearrange("p e h i -> p h i e"), op=ALU.add
+                    )
+                    store(m, a - 1, result)
+
+        quantise_weights(0)
+        quantise_weights(1)
+        for a in range(TOKEN_TILES):
+            nc.vector.quantize_mx(out=x_codes[:, a, :].bitcast(FP8X4), scales=x_scales[:, a, :], in_=x_grouped[a][:])
+        regroup_late(4)
+        quantise_weights(2)
+        quantise_weights(3)
+        project_rotated(0)
+        regroup_late(5)
+        quantise_weights(4)
+        project_plain(1)
+        quantise_weights(5)
+        project_rotated(2)

@@ -30,7 +30,7 @@ HALF_HEAD = HEAD_DIM // 2
 STATS_WIDTH = 512
 STATS_DIM = 6
 QUARTER = WIDTH // 4
-EARLY_CHUNKS = 4
+EARLY_CHUNKS = 3
 
 FLOPS = 2 * TOKENS * D_MODEL * 3 * WIDTH
 
@@ -131,9 +131,11 @@ def tile_transformerlayershard_pa_kernel(
             for quarter in (2, 3):
                 regroup_on_gpsimd(c, quarter)
 
-        def regroup_late(c):
+        def regroup_late_on_scalar(c):
             for quarter in (0, 1, 2):
                 regroup_on_scalar(c, quarter)
+
+        def regroup_late_on_vector(c):
             regroup_on_vector(c, 3)
 
         def quantise_weights(c):
@@ -168,6 +170,7 @@ def tile_transformerlayershard_pa_kernel(
 
         for c in range(1, EARLY_CHUNKS):
             regroup_early(c)
+        regroup_late_on_scalar(EARLY_CHUNKS)
 
         x_grouped = []
         for a in range(TOKEN_TILES):
@@ -250,15 +253,18 @@ def tile_transformerlayershard_pa_kernel(
                     )
                     store(m, a - 1, result)
 
+        regroup_late_on_vector(EARLY_CHUNKS)
         quantise_weights(0)
         quantise_weights(1)
         for a in range(TOKEN_TILES):
             nc.vector.quantize_mx(out=x_codes[:, a, :].bitcast(FP8X4), scales=x_scales[:, a, :], in_=x_grouped[a][:])
-        regroup_late(4)
+        regroup_late_on_scalar(4)
+        regroup_late_on_vector(4)
         quantise_weights(2)
         quantise_weights(3)
         project_rotated(0)
-        regroup_late(5)
+        regroup_late_on_scalar(5)
+        regroup_late_on_vector(5)
         quantise_weights(4)
         project_plain(1)
         quantise_weights(5)

@@ -26,11 +26,11 @@ PACK = 4
 K_PASS = P * PACK
 PASSES = D_MODEL // K_PASS
 BANK = 512
-HALF_HEAD = HEAD_DIM // 2
+PSUM_BANKS = 8
 STATS_WIDTH = 512
 STATS_DIM = 6
-QUARTER = WIDTH // 4
-EARLY_CHUNKS = 3
+HALF = WIDTH // 2
+EARLY_CHUNKS = 4
 
 FLOPS = 2 * TOKENS * D_MODEL * 3 * WIDTH
 
@@ -39,13 +39,16 @@ def tile_transformerlayershard_pa_kernel(
     tc, x, ln_scale, ln_offset, wq, wk, wv, rope_cos, rope_sin, out_0, out_1, out_2
 ):
     nc = tc.nc
-    projections = [(wq, out_0, True), (wv, out_2, False), (wk, out_1, True)]
-    chunks = len(projections) * PASSES
+    weights = [wv, wq, wk]
+    outputs = [out_2, out_0, out_1]
+    rotated_projections = (1, 2)
+    chunks = len(weights) * PASSES
 
     with ExitStack() as stack:
         keep = stack.enter_context(tc.tile_pool(name="keep", bufs=1))
         per_tile = stack.enter_context(tc.tile_pool(name="per_tile", bufs=TOKEN_TILES))
-        banks = stack.enter_context(tc.psum_pool(name="banks", bufs=8))
+        results = stack.enter_context(tc.tile_pool(name="results", bufs=2 * TOKEN_TILES))
+        banks = stack.enter_context(tc.psum_pool(name="banks", bufs=PSUM_BANKS))
         stack.enter_context(tc.manual_schedule())
 
         cos_bf = keep.tile([P, TOKEN_TILES, PAIRS], BF16)
@@ -55,8 +58,8 @@ def tile_transformerlayershard_pa_kernel(
 
         x_rows = x.flatten_outer_dims().rearrange("(p a) d -> p a d", a=TOKEN_TILES)
         x_sb = keep.tile([P, TOKEN_TILES, D_MODEL], BF16)
-        for first in range(0, TOKEN_TILES, 2):
-            nc.sync.dma_start(out=x_sb[:, first : first + 2, :], in_=x_rows[:, first : first + 2, :])
+        for a in range(TOKEN_TILES):
+            nc.sync.dma_start(out=x_sb[:, a, :], in_=x_rows[:, a, :])
 
         affine_rows = keep.tile([P, 2 * D_MODEL], BF16)
         nc.vector.memset(affine_rows[:].bitcast(I32), 0)
@@ -64,14 +67,13 @@ def tile_transformerlayershard_pa_kernel(
         nc.sync.dma_start(out=affine_rows[0:1, D_MODEL : 2 * D_MODEL], in_=ln_offset.rearrange("(o d) -> o d", o=1))
 
         w_raw = []
-        for m, (w, out, rotate) in enumerate(projections):
-            for g in range(PASSES):
-                raw = keep.tile([P, PACK, WIDTH], BF16, name="w_raw_%d_%d" % (m, g))
-                nc.sync.dma_start(
-                    out=raw[:].rearrange("q (u e) n -> q u (e n)", e=2),
-                    in_=w[g * K_PASS : (g + 1) * K_PASS, :].rearrange("(u q e) n -> q u (e n)", u=2, e=2),
-                )
-                w_raw.append(raw)
+        for c in range(chunks):
+            rows = weights[c // PASSES][(c % PASSES) * K_PASS : (c % PASSES + 1) * K_PASS, :]
+            w_raw.append(keep.tile([P, PACK, WIDTH], BF16, name="w_raw_%d" % c))
+            nc.sync.dma_start(
+                out=w_raw[c][:].rearrange("q (u e) n -> q u (e n)", e=2),
+                in_=rows.rearrange("(u q e) n -> q u (e n)", u=2, e=2),
+            )
 
         ones = keep.tile([P, P], BF16)
         nc.vector.memset(ones[:], 1.0)
@@ -81,12 +83,8 @@ def tile_transformerlayershard_pa_kernel(
         identity = keep.tile([P, P], F32)
         make_identity(nc, identity[:])
 
-        cos_or_one = keep.tile([P, TOKEN_TILES, HALF_HEAD], F32)
-        nc.gpsimd.memset(cos_or_one[:], 1.0)
-        nc.gpsimd.tensor_copy(
-            out=cos_or_one[:, :, 0:ROTATED].rearrange("p a (i e) -> p a i e", e=2),
-            in_=cos_bf[:].unsqueeze(3).to_broadcast([P, TOKEN_TILES, PAIRS, 2]),
-        )
+        cos_twice = keep.tile([P, TOKEN_TILES, PAIRS, 2], F32)
+        nc.gpsimd.tensor_copy(out=cos_twice[:], in_=cos_bf[:].unsqueeze(3).to_broadcast([P, TOKEN_TILES, PAIRS, 2]))
         signed_sin = keep.tile([P, TOKEN_TILES, 2, PAIRS], F32)
         nc.gpsimd.tensor_scalar(
             out=signed_sin[:, :, 0, :], in0=sin_bf[:], scalar1=-1.0, scalar2=0.0, op0=ALU.mult, op1=ALU.add
@@ -95,9 +93,10 @@ def tile_transformerlayershard_pa_kernel(
 
         affine_banks = []
         for first in range(0, 2 * D_MODEL, BANK):
-            bank = banks.tile([P, BANK], F32, name="affine_%d" % first, tag="bank")
-            nc.tensor.matmul(out=bank[:], lhsT=ones[:], rhs=affine_rows[:, first : first + BANK], start=True, stop=True)
-            affine_banks.append(bank)
+            affine_banks.append(banks.tile([P, BANK], F32, name="affine_%d" % first, tag="bank"))
+            nc.tensor.matmul(
+                out=affine_banks[-1][:], lhsT=ones[:], rhs=affine_rows[:, first : first + BANK], start=True, stop=True
+            )
         gain_banks = affine_banks[0 : D_MODEL // BANK]
         offset_banks = affine_banks[D_MODEL // BANK :]
 
@@ -107,36 +106,23 @@ def tile_transformerlayershard_pa_kernel(
         for c in range(chunks):
             grouped.append(keep.tile([P, WIDTH, PACK], BF16, name="grouped_%d" % c, align_bytes=64))
 
-        def regroup_views(c, quarter, run):
-            cols = slice(quarter * QUARTER, (quarter + 1) * QUARTER)
+        def regroup_views(c, half, run):
+            cols = slice(half * HALF, (half + 1) * HALF)
             dst = grouped[c][:, cols, :].rearrange("q (n i) t -> q n t i", i=run)
             src = w_raw[c][:, :, cols].rearrange("q t (n i) -> q n t i", i=run)
             return dst, src
 
-        def regroup_on_scalar(c, quarter):
-            dst, src = regroup_views(c, quarter, 4)
+        def regroup_on_scalar(c):
+            dst, src = regroup_views(c, 0, 4)
             nc.scalar.copy(out=dst, in_=src)
 
-        def regroup_on_vector(c, quarter):
-            dst, src = regroup_views(c, quarter, 4)
+        def regroup_on_vector(c):
+            dst, src = regroup_views(c, 1, 4)
             nc.vector.tensor_copy(out=dst, in_=src)
 
-        def regroup_on_gpsimd(c, quarter):
-            dst, src = regroup_views(c, quarter, 1)
+        def regroup_on_gpsimd(c):
+            dst, src = regroup_views(c, 1, 1)
             nc.gpsimd.tensor_scalar(out=dst, in0=src, scalar1=1.0, scalar2=0.0, op0=ALU.mult, op1=ALU.add)
-
-        def regroup_early(c):
-            for quarter in (0, 1):
-                regroup_on_scalar(c, quarter)
-            for quarter in (2, 3):
-                regroup_on_gpsimd(c, quarter)
-
-        def regroup_late_on_scalar(c):
-            for quarter in (0, 1, 2):
-                regroup_on_scalar(c, quarter)
-
-        def regroup_late_on_vector(c):
-            regroup_on_vector(c, 3)
 
         def quantise_weights(c):
             nc.vector.quantize_mx(
@@ -144,7 +130,8 @@ def tile_transformerlayershard_pa_kernel(
                 in_=grouped[c][:].rearrange("q n t -> q (n t)"),
             )
 
-        regroup_early(0)
+        regroup_on_scalar(0)
+        regroup_on_gpsimd(0)
 
         stats = keep.tile([P, TOKEN_TILES, D_MODEL // STATS_WIDTH, STATS_DIM], F32)
         mean_var = keep.tile([P, TOKEN_TILES, 2], F32)
@@ -169,8 +156,8 @@ def tile_transformerlayershard_pa_kernel(
         nc.vector.reciprocal(rstd[:], rstd[:])
 
         for c in range(1, EARLY_CHUNKS):
-            regroup_early(c)
-        regroup_late_on_scalar(EARLY_CHUNKS)
+            regroup_on_scalar(c)
+            regroup_on_gpsimd(c)
 
         x_grouped = []
         for a in range(TOKEN_TILES):
@@ -193,79 +180,62 @@ def tile_transformerlayershard_pa_kernel(
 
         x_codes = keep.tile([P, TOKEN_TILES, PASSES * P], U32, align_bytes=64)
         x_scales = keep.tile([P, TOKEN_TILES, PASSES * P], U8, align_bytes=64)
-
-        def multiply(bank_cols, m, a, first, width):
-            for g in range(PASSES):
-                nc.tensor.matmul_mx(
-                    out=bank_cols,
-                    lhsT=x_codes[:, a, g * P : (g + 1) * P].bitcast(FP8X4),
-                    lhsT_scale=x_scales[:, a, g * P : (g + 1) * P],
-                    rhs=w_codes[:, m * PASSES + g, first : first + width].bitcast(FP8X4),
-                    rhs_scale=w_scales[:, m * PASSES + g, first : first + width],
-                    start=(g == 0),
-                    stop=(g == PASSES - 1),
-                )
-
-        def store(m, a, result):
-            out_rows = projections[m][1].flatten_outer_dims().rearrange(
-                "(p a h) d -> p a (h d)", a=TOKEN_TILES, h=HEADS
-            )
-            nc.sync.dma_start(out=out_rows[:, a, :], in_=result[:].rearrange("p h d -> p (h d)"))
-
-        def project_plain(m):
-            for a in range(TOKEN_TILES):
-                result = per_tile.tile([P, HEADS, HEAD_DIM], F32, name="result")
-                flat = result[:].rearrange("p h d -> p (h d)")
-                for first in range(0, WIDTH, BANK):
-                    bank = banks.tile([P, BANK], F32, tag="bank")
-                    multiply(bank[:], m, a, first, BANK)
-                    nc.scalar.copy(out=flat[:, first : first + BANK], in_=bank[:])
-                store(m, a, result)
-
-        def project_rotated(m):
-            products = []
-            for a in range(TOKEN_TILES + 1):
-                if a < TOKEN_TILES:
-                    leading = banks.tile([P, HEADS, HALF_HEAD], F32, tag="bank")
-                    trailing = banks.tile([P, HEADS, HALF_HEAD], F32, tag="bank")
-                    for h in range(HEADS):
-                        multiply(leading[:, h, :], m, a, h * HEAD_DIM, HALF_HEAD)
-                        multiply(trailing[:, h, :], m, a, h * HEAD_DIM + HALF_HEAD, HALF_HEAD)
-                    result = per_tile.tile([P, HEADS, HEAD_DIM], F32, name="result")
-                    cross = per_tile.tile([P, 2, HEADS, PAIRS], F32, name="cross")
-                    nc.scalar.copy(out=result[:, :, HALF_HEAD:HEAD_DIM], in_=trailing[:])
-                    nc.vector.tensor_tensor(
-                        out=result[:, :, 0:HALF_HEAD], in0=leading[:],
-                        in1=cos_or_one[:, a, :].unsqueeze(1).to_broadcast([P, HEADS, HALF_HEAD]), op=ALU.mult,
-                    )
-                    u_pairs = leading[:, :, 0:ROTATED].rearrange("p h (i e) -> p h i e", e=2)
-                    for e in range(2):
-                        nc.vector.tensor_tensor(
-                            out=cross[:, e, :, :], in0=u_pairs[:, :, :, 1 - e],
-                            in1=signed_sin[:, a, e, :].unsqueeze(1).to_broadcast([P, HEADS, PAIRS]), op=ALU.mult,
-                        )
-                    products.append((result, cross))
-                if a > 0:
-                    result, cross = products[a - 1]
-                    rotated = result[:, :, 0:ROTATED].rearrange("p h (i e) -> p h i e", e=2)
-                    nc.vector.tensor_tensor(
-                        out=rotated, in0=rotated, in1=cross[:].rearrange("p e h i -> p h i e"), op=ALU.add
-                    )
-                    store(m, a - 1, result)
-
-        regroup_late_on_vector(EARLY_CHUNKS)
         quantise_weights(0)
         quantise_weights(1)
         for a in range(TOKEN_TILES):
             nc.vector.quantize_mx(out=x_codes[:, a, :].bitcast(FP8X4), scales=x_scales[:, a, :], in_=x_grouped[a][:])
-        regroup_late_on_scalar(4)
-        regroup_late_on_vector(4)
-        quantise_weights(2)
-        quantise_weights(3)
-        project_rotated(0)
-        regroup_late_on_scalar(5)
-        regroup_late_on_vector(5)
-        quantise_weights(4)
-        project_plain(1)
-        quantise_weights(5)
-        project_rotated(2)
+        for c in range(EARLY_CHUNKS, chunks):
+            regroup_on_scalar(c)
+            regroup_on_vector(c)
+            quantise_weights(c - 2)
+        for c in range(chunks - 2, chunks):
+            quantise_weights(c)
+
+        result = {}
+        for m in range(len(weights)):
+            out_rows = outputs[m].flatten_outer_dims().rearrange("(p a h) d -> p a (h d)", a=TOKEN_TILES, h=HEADS)
+            for a in range(TOKEN_TILES):
+                result[m, a] = results.tile([P, WIDTH], F32, name="result")
+                for first in range(0, WIDTH, BANK):
+                    bank = banks.tile([P, BANK], F32, tag="bank")
+                    for g in range(PASSES):
+                        nc.tensor.matmul_mx(
+                            out=bank[:],
+                            lhsT=x_codes[:, a, g * P : (g + 1) * P].bitcast(FP8X4),
+                            lhsT_scale=x_scales[:, a, g * P : (g + 1) * P],
+                            rhs=w_codes[:, m * PASSES + g, first : first + BANK].bitcast(FP8X4),
+                            rhs_scale=w_scales[:, m * PASSES + g, first : first + BANK],
+                            start=(g == 0),
+                            stop=(g == PASSES - 1),
+                        )
+                    nc.scalar.copy(out=result[m, a][:, first : first + BANK], in_=bank[:])
+                if m not in rotated_projections:
+                    nc.sync.dma_start(out=out_rows[:, a, :], in_=result[m, a][:])
+
+        to_rotate = [(m, a) for m in rotated_projections for a in range(TOKEN_TILES)]
+        cross = {}
+        for j in range(len(to_rotate) + 1):
+            if j < len(to_rotate):
+                m, a = to_rotate[j]
+                u = result[m, a][:].rearrange("p (h d) -> p h d", h=HEADS)[:, :, 0:ROTATED]
+                u_pairs = u.rearrange("p h (i e) -> p h i e", e=2)
+                cross[m, a] = per_tile.tile([P, 2, HEADS, PAIRS], F32, name="cross")
+                for e in range(2):
+                    nc.vector.tensor_tensor(
+                        out=cross[m, a][:, e, :, :], in0=u_pairs[:, :, :, 1 - e],
+                        in1=signed_sin[:, a, e, :].unsqueeze(1).to_broadcast([P, HEADS, PAIRS]), op=ALU.mult,
+                    )
+                nc.vector.tensor_tensor(
+                    out=u, in0=u,
+                    in1=cos_twice[:, a, :, :].rearrange("p i e -> p (i e)").unsqueeze(1).to_broadcast([P, HEADS, ROTATED]),
+                    op=ALU.mult,
+                )
+            if j > 0:
+                m, a = to_rotate[j - 1]
+                u = result[m, a][:].rearrange("p (h d) -> p h d", h=HEADS)[:, :, 0:ROTATED]
+                u_pairs = u.rearrange("p h (i e) -> p h i e", e=2)
+                nc.vector.tensor_tensor(
+                    out=u_pairs, in0=u_pairs, in1=cross[m, a][:].rearrange("p e h i -> p h i e"), op=ALU.add
+                )
+                out_rows = outputs[m].flatten_outer_dims().rearrange("(p a h) d -> p a (h d)", a=TOKEN_TILES, h=HEADS)
+                nc.sync.dma_start(out=out_rows[:, a, :], in_=result[m, a][:])

from contextlib import ExitStack

import concourse.mybir as mybir
from concourse.masks import make_identity

F32 = mybir.dt.float32
BF16 = mybir.dt.bfloat16
I32 = mybir.dt.int32
U32 = mybir.dt.uint32
U8 = mybir.dt.uint8
FP8X4 = mybir.dt.float8_e4m3fn_x4
ALU = mybir.AluOpType

P = 128
TOKENS = 512
D_MODEL = 1024
HEADS = 4
HEAD_DIM = 256
ROTATED = 64
PAIRS = ROTATED // 2
WIDTH = HEADS * HEAD_DIM
EPS = 1e-5

TOKEN_TILES = TOKENS // P
PACK = 4
K_PASS = P * PACK
PASSES = D_MODEL // K_PASS
BANK = 512
PSUM_BANKS = 8
STATS_WIDTH = 512
STATS_DIM = 6
HALF = WIDTH // 2
EARLY_CHUNKS = 4

FLOPS = 2 * TOKENS * D_MODEL * 3 * WIDTH


def tile_transformerlayershard_pa_kernel(
    tc, x, ln_scale, ln_offset, wq, wk, wv, rope_cos, rope_sin, out_0, out_1, out_2
):
    nc = tc.nc
    weights = [wv, wq, wk]
    outputs = [out_2, out_0, out_1]
    rotated_projections = (1, 2)
    chunks = len(weights) * PASSES

    with ExitStack() as stack:
        keep = stack.enter_context(tc.tile_pool(name="keep", bufs=1))
        per_tile = stack.enter_context(tc.tile_pool(name="per_tile", bufs=TOKEN_TILES))
        results = stack.enter_context(tc.tile_pool(name="results", bufs=2 * TOKEN_TILES))
        banks = stack.enter_context(tc.psum_pool(name="banks", bufs=PSUM_BANKS))
        stack.enter_context(tc.manual_schedule())

        cos_bf = keep.tile([P, TOKEN_TILES, PAIRS], BF16)
        sin_bf = keep.tile([P, TOKEN_TILES, PAIRS], BF16)
        nc.scalar.dma_start(out=cos_bf[:], in_=rope_cos.rearrange("(p a) i -> p a i", a=TOKEN_TILES))
        nc.scalar.dma_start(out=sin_bf[:], in_=rope_sin.rearrange("(p a) i -> p a i", a=TOKEN_TILES))

        x_rows = x.flatten_outer_dims().rearrange("(p a) d -> p a d", a=TOKEN_TILES)
        x_sb = keep.tile([P, TOKEN_TILES, D_MODEL], BF16)
        for a in range(TOKEN_TILES):
            nc.sync.dma_start(out=x_sb[:, a, :], in_=x_rows[:, a, :])

        affine_rows = keep.tile([P, 2 * D_MODEL], BF16)
        nc.vector.memset(affine_rows[:].bitcast(I32), 0)
        nc.sync.dma_start(out=affine_rows[0:1, 0:D_MODEL], in_=ln_scale.rearrange("(o d) -> o d", o=1))
        nc.sync.dma_start(out=affine_rows[0:1, D_MODEL : 2 * D_MODEL], in_=ln_offset.rearrange("(o d) -> o d", o=1))

        w_raw = []
        for c in range(chunks):
            rows = weights[c // PASSES][(c % PASSES) * K_PASS : (c % PASSES + 1) * K_PASS, :]
            w_raw.append(keep.tile([P, PACK, WIDTH], BF16, name="w_raw_%d" % c))
            nc.sync.dma_start(
                out=w_raw[c][:].rearrange("q (u e) n -> q u (e n)", e=2),
                in_=rows.rearrange("(u q e) n -> q u (e n)", u=2, e=2),
            )

        ones = keep.tile([P, P], BF16)
        nc.vector.memset(ones[:], 1.0)
        warm = keep.tile([P, 1], F32)
        nc.vector.memset(warm[:], 1.0)
        nc.scalar.sqrt(warm[:], warm[:])
        identity = keep.tile([P, P], F32)
        make_identity(nc, identity[:])

        cos_twice = keep.tile([P, TOKEN_TILES, PAIRS, 2], F32)
        nc.gpsimd.tensor_copy(out=cos_twice[:], in_=cos_bf[:].unsqueeze(3).to_broadcast([P, TOKEN_TILES, PAIRS, 2]))
        signed_sin = keep.tile([P, TOKEN_TILES, 2, PAIRS], F32)
        nc.gpsimd.tensor_scalar(
            out=signed_sin[:, :, 0, :], in0=sin_bf[:], scalar1=-1.0, scalar2=0.0, op0=ALU.mult, op1=ALU.add
        )
        nc.gpsimd.tensor_copy(out=signed_sin[:, :, 1, :], in_=sin_bf[:])

        affine_banks = []
        for first in range(0, 2 * D_MODEL, BANK):
            affine_banks.append(banks.tile([P, BANK], F32, name="affine_%d" % first, tag="bank"))
            nc.tensor.matmul(
                out=affine_banks[-1][:], lhsT=ones[:], rhs=affine_rows[:, first : first + BANK], start=True, stop=True
            )
        gain_banks = affine_banks[0 : D_MODEL // BANK]
        offset_banks = affine_banks[D_MODEL // BANK :]

        w_codes = keep.tile([P, chunks, WIDTH], U32, align_bytes=64)
        w_scales = keep.tile([P, chunks, WIDTH], U8, align_bytes=64)
        grouped = []
        for c in range(chunks):
            grouped.append(keep.tile([P, WIDTH, PACK], BF16, name="grouped_%d" % c, align_bytes=64))

        def regroup_views(c, half, run):
            cols = slice(half * HALF, (half + 1) * HALF)
            dst = grouped[c][:, cols, :].rearrange("q (n i) t -> q n t i", i=run)
            src = w_raw[c][:, :, cols].rearrange("q t (n i) -> q n t i", i=run)
            return dst, src

        def regroup_on_scalar(c):
            dst, src = regroup_views(c, 0, 4)
            nc.scalar.copy(out=dst, in_=src)

        def regroup_on_vector(c):
            dst, src = regroup_views(c, 1, 4)
            nc.vector.tensor_copy(out=dst, in_=src)

        def regroup_on_gpsimd(c):
            dst, src = regroup_views(c, 1, 1)
            nc.gpsimd.tensor_scalar(out=dst, in0=src, scalar1=1.0, scalar2=0.0, op0=ALU.mult, op1=ALU.add)

        def quantise_weights(c):
            nc.vector.quantize_mx(
                out=w_codes[:, c, :].bitcast(FP8X4), scales=w_scales[:, c, :],
                in_=grouped[c][:].rearrange("q n t -> q (n t)"),
            )

        regroup_on_scalar(0)
        regroup_on_gpsimd(0)

        stats = keep.tile([P, TOKEN_TILES, D_MODEL // STATS_WIDTH, STATS_DIM], F32)
        mean_var = keep.tile([P, TOKEN_TILES, 2], F32)
        for a in range(TOKEN_TILES):
            for s in range(D_MODEL // STATS_WIDTH):
                nc.vector.bn_stats(out=stats[:, a, s, :], in_=x_sb[:, a, s * STATS_WIDTH : (s + 1) * STATS_WIDTH])
        for a in range(TOKEN_TILES):
            nc.vector.bn_aggr(out=mean_var[:, a, :], in_=stats[:, a, :, :].rearrange("p s v -> p (s v)"))
        rstd = keep.tile([P, TOKEN_TILES], F32)
        nc.vector.tensor_scalar(out=rstd[:], in0=mean_var[:, :, 1], scalar1=EPS, scalar2=None, op0=ALU.add)
        nc.scalar.sqrt(rstd[:], rstd[:])

        centred = []
        for a in range(TOKEN_TILES):
            centred.append(per_tile.tile([P, D_MODEL], F32, name="centred"))
            for h, first in enumerate(range(0, D_MODEL, BANK)):
                cols = slice(first, first + BANK)
                nc.vector.scalar_tensor_tensor(
                    out=centred[a][:, cols], in0=x_sb[:, a, cols], scalar=mean_var[:, a, 0:1],
                    in1=gain_banks[h][:], op0=ALU.subtract, op1=ALU.mult,
                )
        nc.vector.reciprocal(rstd[:], rstd[:])

        for c in range(1, EARLY_CHUNKS):
            regroup_on_scalar(c)
            regroup_on_gpsimd(c)

        x_grouped = []
        for a in range(TOKEN_TILES):
            xn = per_tile.tile([P, D_MODEL], BF16)
            for h, first in enumerate(range(0, D_MODEL, BANK)):
                cols = slice(first, first + BANK)
                nc.vector.scalar_tensor_tensor(
                    out=xn[:, cols], in0=centred[a][:, cols], scalar=rstd[:, a : a + 1],
                    in1=offset_banks[h][:], op0=ALU.mult, op1=ALU.add,
                )
            xn_words = xn[:].bitcast(F32)
            xt = banks.tile([P, PASSES * 2, P], F32, tag="bank")
            for b in range(PASSES * 2):
                nc.tensor.transpose(out=xt[:, b, :], in_=xn_words[:, b * P : (b + 1) * P], identity=identity[:])
            x_grouped.append(per_tile.tile([P, PASSES * P * PACK], BF16, name="x_grouped", align_bytes=64))
            nc.scalar.copy(
                out=x_grouped[a][:].bitcast(F32).rearrange("q (g r u) -> q g r u", g=PASSES, u=2),
                in_=xt[:].rearrange("q (g u) r -> q g r u", u=2),
            )

        x_codes = keep.tile([P, TOKEN_TILES, PASSES * P], U32, align_bytes=64)
        x_scales = keep.tile([P, TOKEN_TILES, PASSES * P], U8, align_bytes=64)
        quantise_weights(0)
        quantise_weights(1)
        for a in range(TOKEN_TILES):
            nc.vector.quantize_mx(out=x_codes[:, a, :].bitcast(FP8X4), scales=x_scales[:, a, :], in_=x_grouped[a][:])
        for c in range(EARLY_CHUNKS, chunks):
            regroup_on_scalar(c)
            regroup_on_vector(c)
            quantise_weights(c - 2)
        for c in range(chunks - 2, chunks):
            quantise_weights(c)

        result = {}
        for m in range(len(weights)):
            out_rows = outputs[m].flatten_outer_dims().rearrange("(p a h) d -> p a (h d)", a=TOKEN_TILES, h=HEADS)
            for a in range(TOKEN_TILES):
                result[m, a] = results.tile([P, WIDTH], F32, name="result")
                for first in range(0, WIDTH, BANK):
                    bank = banks.tile([P, BANK], F32, tag="bank")
                    for g in range(PASSES):
                        nc.tensor.matmul_mx(
                            out=bank[:],
                            lhsT=x_codes[:, a, g * P : (g + 1) * P].bitcast(FP8X4),
                            lhsT_scale=x_scales[:, a, g * P : (g + 1) * P],
                            rhs=w_codes[:, m * PASSES + g, first : first + BANK].bitcast(FP8X4),
                            rhs_scale=w_scales[:, m * PASSES + g, first : first + BANK],
                            start=(g == 0),
                            stop=(g == PASSES - 1),
                        )
                    nc.scalar.copy(out=result[m, a][:, first : first + BANK], in_=bank[:])
                if m not in rotated_projections:
                    nc.sync.dma_start(out=out_rows[:, a, :], in_=result[m, a][:])

        to_rotate = [(m, a) for m in rotated_projections for a in range(TOKEN_TILES)]
        cross = {}
        for j in range(len(to_rotate) + 1):
            if j < len(to_rotate):
                m, a = to_rotate[j]
                u = result[m, a][:].rearrange("p (h d) -> p h d", h=HEADS)[:, :, 0:ROTATED]
                u_pairs = u.rearrange("p h (i e) -> p h i e", e=2)
                cross[m, a] = per_tile.tile([P, 2, HEADS, PAIRS], F32, name="cross")
                for e in range(2):
                    nc.vector.tensor_tensor(
                        out=cross[m, a][:, e, :, :], in0=u_pairs[:, :, :, 1 - e],
                        in1=signed_sin[:, a, e, :].unsqueeze(1).to_broadcast([P, HEADS, PAIRS]), op=ALU.mult,
                    )
                nc.vector.tensor_tensor(
                    out=u, in0=u,
                    in1=cos_twice[:, a, :, :].rearrange("p i e -> p (i e)").unsqueeze(1).to_broadcast([P, HEADS, ROTATED]),
                    op=ALU.mult,
                )
            if j > 0:
                m, a = to_rotate[j - 1]
                u = result[m, a][:].rearrange("p (h d) -> p h d", h=HEADS)[:, :, 0:ROTATED]
                u_pairs = u.rearrange("p h (i e) -> p h i e", e=2)
                nc.vector.tensor_tensor(
                    out=u_pairs, in0=u_pairs, in1=cross[m, a][:].rearrange("p e h i -> p h i e"), op=ALU.add
                )
                out_rows = outputs[m].flatten_outer_dims().rearrange("(p a h) d -> p a (h d)", a=TOKEN_TILES, h=HEADS)
                nc.sync.dma_start(out=out_rows[:, a, :], in_=result[m, a][:])
